import numpy as np
import ml_dtypes


def mxq(x, axis, fmt="e4m3"):
    dtype, down = {"e4m3": (ml_dtypes.float8_e4m3fn, 7), "e5m2": (ml_dtypes.float8_e5m2, 14)}[fmt]
    v = np.moveaxis(np.asarray(x, np.float32).astype(ml_dtypes.bfloat16).astype(np.float64), axis, -1)
    blocks = v.reshape(v.shape[:-1] + (-1, 32))
    amax = np.abs(blocks).max(-1, keepdims=True)
    byte = np.maximum(np.where(amax > 0, np.frexp(amax)[1] - 1 + 127, 0) - down, 1)
    scale = np.exp2(byte - 127.0)
    codes = (blocks / scale).astype(np.float32).astype(dtype).astype(np.float64)
    return np.moveaxis((codes * scale).reshape(v.shape), -1, axis)


WIDE = False


def mx_kscale(k):
    if not WIDE:
        return np.ones(k)
    levels = np.array([10, -10, 5, -5, 0])
    a = np.random.permutation(np.resize(levels, k // 512 * 4)).reshape(k // 512, 4)
    idx = np.arange(k)
    return np.exp2(a[idx // 512, idx % 128 // 32])


BF16 = ml_dtypes.bfloat16


def bf(x):
    return np.asarray(x, np.float32).astype(BF16)


def f64(x):
    return np.asarray(x).astype(np.float64)


B, G, Z1, Z2, H, PD = 256, 16, 256, 256, 512, 512


def glin(x, W, b):
    y = mxq(x, 2, "e4m3").transpose(1, 0, 2) @ mxq(f64(W), 2, "e4m3").transpose(0, 2, 1)
    return y.transpose(1, 0, 2) + f64(b)


def setup_inputs():
    s = mx_kscale(H)
    h = np.maximum(np.random.standard_normal((B, G, H)), 0.0) + np.maximum(np.random.standard_normal((B, G, H)), 0.0)
    return {"h": bf(h * s),
            "W3": bf(np.random.standard_normal((G, H, H)) / np.sqrt(H) * s[None, :, None] / s[None, None, :]),
            "b3": bf(np.random.standard_normal((G, H)) * 0.2 * s),
            "Wo": bf(np.random.standard_normal((G, PD, H)) * 0.6 / np.sqrt(H) / s[None, None, :]),
            "bo": bf(np.random.standard_normal((G, PD)) * 0.2)}


def reference(h, W3, b3, Wo, bo):
    h = f64(h)
    h3 = np.maximum(glin(h, W3, b3), 0.0) + h
    out = glin(h3, Wo, bo)
    return out.reshape(B, G * PD)

@@ -1,0 +1,242 @@
+from contextlib import ExitStack
+
+import concourse.mybir as mybir
+from concourse.masks import make_identity
+
+F32 = mybir.dt.float32
+BF16 = mybir.dt.bfloat16
+U32 = mybir.dt.uint32
+U8 = mybir.dt.uint8
+FP8X4 = mybir.dt.float8_e4m3fn_x4
+ADD = mybir.AluOpType.add
+RELU = mybir.ActivationFunctionType.Relu
+
+P = 128
+B, G, H, PD = 256, 16, 512, 512
+FLOPS = 2 * B * G * H * (H + PD)
+
+W_BUFS = 8
+LOOKAHEAD = W_BUFS - 1
+H_CHUNKS = ((0, 2), (2, 4), (4, 8), (8, 12), (12, 16))
+
+
+def tile_linearwdecoder_pb_kernel(tc, h, W3, b3, Wo, bo, out):
+    nc = tc.nc
+    with ExitStack() as ctx:
+        const = ctx.enter_context(tc.tile_pool(name="const", bufs=1))
+        wnat = ctx.enter_context(tc.tile_pool(name="wnat", bufs=W_BUFS))
+        grp = ctx.enter_context(tc.tile_pool(name="grp", bufs=2))
+        cod = ctx.enter_context(tc.tile_pool(name="cod", bufs=2))
+        res = ctx.enter_context(tc.tile_pool(name="res", bufs=2))
+        tp = ctx.enter_context(tc.psum_pool(name="tp", bufs=4))
+        xp = ctx.enter_context(tc.psum_pool(name="xp", bufs=2))
+        yp = ctx.enter_context(tc.psum_pool(name="yp", bufs=2))
+        ctx.enter_context(tc.manual_schedule())
+
+        w3_view = W3.rearrange("g (u q e) k -> q g u (e k)", u=2, q=P, e=2)
+        wo_view = Wo.rearrange("g (q r) k -> q g (r k)", r=4)
+        h_view = h.rearrange("(bb m) g k -> m bb (g k)", m=P)
+        out_view = out.rearrange("(bb m) c -> m bb c", m=P)
+
+        b3n = const.tile([P, 256], BF16)
+        bo16 = const.tile([P, PD], BF16)
+        nc.vector.memset(b3n[:], 0.0)
+        nc.vector.memset(bo16[:], 0.0)
+        nc.scalar.dma_start(out=b3n[0:32, :], in_=b3.rearrange("g (u w) -> (g u) w", u=2))
+        nc.scalar.dma_start(out=bo16[0:G, :], in_=bo)
+        ident = const.tile([P, P], F32)
+        make_identity(nc, ident[:])
+        identb = const.tile([P, P], BF16)
+        make_identity(nc, identb[:])
+        b3c = const.tile([P, 4 * G], F32)
+        bo_bc = const.tile([P, G * PD], BF16)
+
+        h_tiles = {}
+        w3n = {}
+        won = {}
+
+        def load_h(c):
+            g0, g1 = H_CHUNKS[c]
+            t = const.tile([P, 2 * (g1 - g0) * H], BF16, name="hnat%d" % c)
+            nc.sync.dma_start(
+                out=t[:].rearrange("p (bb x) -> p bb x", bb=2),
+                in_=h_view[:, :, g0 * H : g1 * H],
+            )
+            for g in range(g0, g1):
+                h_tiles[g] = (t, g1 - g0, g - g0)
+
+        def load_w(g):
+            a = wnat.tile([P, 4 * H], BF16, tag="w3n", name="w3n")
+            nc.sync.dma_start(out=a[:].rearrange("p (u x) -> p u x", u=2), in_=w3_view[:, g])
+            w3n[g] = a
+            for c in range(len(H_CHUNKS)):
+                if H_CHUNKS[c][0] == g:
+                    load_h(c)
+            b = wnat.tile([P, 4 * H], BF16, tag="won", name="won")
+            nc.sync.dma_start(out=b[:], in_=wo_view[:, g])
+            won[g] = b
+
+        w3g, wog, hg, h3g = {}, {}, {}, {}
+        w3c, woc, hc, h3c = {}, {}, {}, {}
+        xs, rs, ots = {}, {}, {}
+
+        def flip(words, offsets, dst_words):
+            bank = tp.tile([P, 512], F32, tag="tp", name="bank")
+            for i in range(4):
+                nc.tensor.transpose(
+                    bank[:, 128 * i : 128 * i + 128], words[:, offsets[i] : offsets[i] + 128], ident[:]
+                )
+            nc.scalar.copy(
+                out=dst_words.rearrange("p (a q u) -> p a q u", a=2, u=2),
+                in_=bank[:].rearrange("p (a u q) -> p a q u", a=2, u=2),
+            )
+
+        def transposes(g):
+            a = grp.tile([P, 4 * H], BF16, tag="w3g", name="w3g", align_bytes=64)
+            w3g[g] = a
+            src = w3n[g][:].bitcast(F32)
+            for half in range(2):
+                flip(src, [512 * half + 128 * i for i in range(4)], a[:].bitcast(F32)[:, 512 * half : 512 * half + 512])
+            t, ng, gi = h_tiles[g]
+            c = grp.tile([P, 4 * B], BF16, tag="hg", name="hg", align_bytes=64, bufs=3)
+            hg[g] = c
+            flip(
+                t[:].bitcast(F32),
+                [(bb * ng + gi) * 256 + 128 * u for bb in range(2) for u in range(2)],
+                c[:].bitcast(F32),
+            )
+            b = grp.tile([P, 4 * PD], BF16, tag="wog", name="wog", align_bytes=64)
+            wog[g] = b
+            src = won[g][:].bitcast(F32)
+            for half in range(2):
+                flip(src, [512 * half + 128 * i for i in range(4)], b[:].bitcast(F32)[:, 512 * half : 512 * half + 512])
+
+        def spread_bias(c):
+            bank = tp.tile([P, 1024], BF16, tag="tp", name="bbank")
+            for i in range(2):
+                g = 2 * c + i
+                nc.tensor.matmul(
+                    bank[:, 512 * i : 512 * i + 512],
+                    lhsT=identb[:, g : g + 1].to_broadcast([P, P]),
+                    rhs=bo16[:],
+                    start=True,
+                    stop=True,
+                )
+            nc.scalar.copy(out=bo_bc[:, 1024 * c : 1024 * c + 1024], in_=bank[:])
+
+        def quantise(src, width, tag):
+            codes = cod.tile([P, width], U32, tag=tag + "c", name=tag + "c", align_bytes=64)
+            scales = cod.tile([P, width], U8, tag=tag + "s", name=tag + "s", align_bytes=64)
+            nc.vector.quantize_mx(out=codes[:].bitcast(FP8X4), scales=scales[:], in_=src[:])
+            return codes, scales
+
+        def mm1(g):
+            wc, ws = w3c[g]
+            ac, as_ = hc[g]
+            banks = []
+            for half in range(2):
+                x = xp.tile([P, 512], F32, tag="x", name="x")
+                banks.append(x)
+                for i in range(2):
+                    t = 2 * half + i
+                    nc.tensor.matmul_mx(
+                        out=x[:, 256 * i : 256 * i + 256],
+                        lhsT=wc[:, 128 * t : 128 * t + 128].bitcast(FP8X4),
+                        lhsT_scale=ws[:, 128 * t : 128 * t + 128],
+                        rhs=ac[:].bitcast(FP8X4),
+                        rhs_scale=as_[:],
+                        start=True,
+                        stop=True,
+                    )
+            xs[g] = banks
+
+        def relu(g):
+            r = res.tile([P, 4 * B], F32, tag="r", name="r")
+            rs[g] = r
+            banks = xs[g]
+            for t in range(4):
+                nc.scalar.activation(
+                    out=r[:, 256 * t : 256 * t + 256],
+                    in_=banks[t // 2][:, 256 * (t % 2) : 256 * (t % 2) + 256],
+                    func=RELU,
+                    bias=b3c[:, 4 * g + t : 4 * g + t + 1],
+                    scale=1.0,
+                )
+
+        def residual(g):
+            s = grp.tile([P, 4 * B], BF16, tag="h3g", name="h3g", align_bytes=64)
+            h3g[g] = s
+            nc.vector.tensor_tensor(
+                out=s[:].rearrange("p (b t) -> p b t", t=4),
+                in0=rs[g][:].rearrange("p (t b) -> p b t", t=4),
+                in1=hg[g][:].rearrange("p (b t) -> p b t", t=4),
+                op=ADD,
+            )
+
+        def mm2_and_bias(g):
+            ac, as_ = h3c[g]
+            wc, ws = woc[g]
+            if g % 2 == 0:
+                ots[g // 2] = res.tile([P, 2 * 2 * PD], F32, tag="ot", name="ot", bufs=3)
+            ot = ots[g // 2][:].rearrange("p (bb c) -> p bb c", bb=2)
+            ys = []
+            for bb in range(2):
+                y = yp.tile([P, PD], F32, tag="y", name="y")
+                ys.append(y)
+                nc.tensor.matmul_mx(
+                    out=y[:],
+                    lhsT=ac[:, 128 * bb : 128 * bb + 128].bitcast(FP8X4),
+                    lhsT_scale=as_[:, 128 * bb : 128 * bb + 128],
+                    rhs=wc[:].bitcast(FP8X4),
+                    rhs_scale=ws[:],
+                    start=True,
+                    stop=True,
+                )
+            c0 = PD * (g % 2)
+            for bb in range(2):
+                nc.vector.tensor_tensor(
+                    out=ot[:, bb, c0 : c0 + PD].rearrange("p (q r) -> p q r", r=4),
+                    in0=ys[bb][:].rearrange("p (r q) -> p q r", r=4),
+                    in1=bo_bc[:, PD * g : PD * g + PD].rearrange("p (q r) -> p q r", r=4),
+                    op=ADD,
+                )
+
+        def store(g0, g1):
+            ot = ots[g0 // 2][:].rearrange("p (bb c) -> p bb c", bb=2)
+            c0 = PD * (g0 % 2)
+            nc.sync.dma_start(
+                out=out_view[:, :, PD * g0 : PD * g1], in_=ot[:, :, c0 : c0 + PD * (g1 - g0)]
+            )
+
+        for g in range(LOOKAHEAD):
+            load_w(g)
+        bank = tp.tile([P, 512], F32, tag="tp", name="b3bank")
+        nc.tensor.transpose(bank[:, 0:128], b3n[:].bitcast(F32), ident[:])
+        nc.vector.tensor_copy(out=b3c[:], in_=bank[:, 0 : 2 * G].bitcast(BF16))
+        spread_bias(0)
+
+        for j in range(G + 3):
+            if j + LOOKAHEAD < G:
+                load_w(j + LOOKAHEAD)
+            g = j - 3
+            if 0 <= g < G - 2 and g % 2 == 1:
+                store(g - 1, g + 1)
+            if g >= G - 2:
+                store(g, g + 1)
+            if 0 <= j - 2 < G:
+                residual(j - 2)
+            if 0 <= j - 1 < G:
+                woc[j - 1] = quantise(wog[j - 1], PD, "wo")
+            if 0 <= j - 2 < G:
+                h3c[j - 2] = quantise(h3g[j - 2], B, "h3")
+            if j < G:
+                transposes(j)
+                if j % 2 == 0 and j + 2 < G:
+                    spread_bias(j // 2 + 1)
+                w3c[j] = quantise(w3g[j], H, "w3")
+                hc[j] = quantise(hg[j], B, "h")
+            if 0 <= j - 1 < G:
+                mm1(j - 1)
+                relu(j - 1)
+            if 0 <= j - 2 < G:
+                mm2_and_bias(j - 2)

@@ -17,6 +17,7 @@ FLOPS = 2 * B * G * H * (H + PD)
 
 W_BUFS = 8
 LOOKAHEAD = W_BUFS - 1
+HEAD_BIAS = {0: (1, 2, 3), 1: (4, 5, 6), 2: (7,)}
 H_CHUNKS = ((0, 2), (2, 4), (4, 8), (8, 12), (12, 16))
 
 
@@ -42,8 +43,8 @@ def tile_linearwdecoder_pb_kernel(tc, h, W3, b3, Wo, bo, out):
         bo16 = const.tile([P, PD], BF16)
         nc.vector.memset(b3n[:], 0.0)
         nc.vector.memset(bo16[:], 0.0)
-        nc.scalar.dma_start(out=b3n[0:32, :], in_=b3.rearrange("g (u w) -> (g u) w", u=2))
-        nc.scalar.dma_start(out=bo16[0:G, :], in_=bo)
+        nc.sync.dma_start(out=bo16[0:G, :], in_=bo)
+        nc.sync.dma_start(out=b3n[0:32, :], in_=b3.rearrange("g (u w) -> (g u) w", u=2))
         ident = const.tile([P, P], F32)
         make_identity(nc, ident[:])
         identb = const.tile([P, P], BF16)
@@ -78,7 +79,7 @@ def tile_linearwdecoder_pb_kernel(tc, h, W3, b3, Wo, bo, out):
 
         w3g, wog, hg, h3g = {}, {}, {}, {}
         w3c, woc, hc, h3c = {}, {}, {}, {}
-        xs, rs, ots = {}, {}, {}
+        xs, rs, ys, ots = {}, {}, {}, {}
 
         def flip(words, offsets, dst_words):
             bank = tp.tile([P, 512], F32, tag="tp", name="bank")
@@ -91,12 +92,16 @@ def tile_linearwdecoder_pb_kernel(tc, h, W3, b3, Wo, bo, out):
                 in_=bank[:].rearrange("p (a u q) -> p a q u", a=2, u=2),
             )
 
-        def transposes(g):
+        def transposes(g, extra):
             a = grp.tile([P, 4 * H], BF16, tag="w3g", name="w3g", align_bytes=64)
             w3g[g] = a
             src = w3n[g][:].bitcast(F32)
             for half in range(2):
                 flip(src, [512 * half + 128 * i for i in range(4)], a[:].bitcast(F32)[:, 512 * half : 512 * half + 512])
+            if g == 0:
+                bias3_to_partitions()
+            if len(extra) > 0:
+                spread_bias(extra[0])
             t, ng, gi = h_tiles[g]
             c = grp.tile([P, 4 * B], BF16, tag="hg", name="hg", align_bytes=64, bufs=3)
             hg[g] = c
@@ -105,11 +110,20 @@ def tile_linearwdecoder_pb_kernel(tc, h, W3, b3, Wo, bo, out):
                 [(bb * ng + gi) * 256 + 128 * u for bb in range(2) for u in range(2)],
                 c[:].bitcast(F32),
             )
+            if len(extra) > 1:
+                spread_bias(extra[1])
             b = grp.tile([P, 4 * PD], BF16, tag="wog", name="wog", align_bytes=64)
             wog[g] = b
             src = won[g][:].bitcast(F32)
             for half in range(2):
                 flip(src, [512 * half + 128 * i for i in range(4)], b[:].bitcast(F32)[:, 512 * half : 512 * half + 512])
+            if len(extra) > 2:
+                spread_bias(extra[2])
+
+        def bias3_to_partitions():
+            bank = tp.tile([P, 512], F32, tag="tp", name="b3bank")
+            nc.tensor.transpose(bank[:, 0:128], b3n[:].bitcast(F32), ident[:])
+            nc.vector.tensor_copy(out=b3c[:], in_=bank[:, 0 : 2 * G].bitcast(BF16))
 
         def spread_bias(c):
             bank = tp.tile([P, 1024], BF16, tag="tp", name="bbank")
@@ -122,7 +136,7 @@ def tile_linearwdecoder_pb_kernel(tc, h, W3, b3, Wo, bo, out):
                     start=True,
                     stop=True,
                 )
-            nc.scalar.copy(out=bo_bc[:, 1024 * c : 1024 * c + 1024], in_=bank[:])
+            nc.vector.tensor_copy(out=bo_bc[:, 1024 * c : 1024 * c + 1024], in_=bank[:])
 
         def quantise(src, width, tag):
             codes = cod.tile([P, width], U32, tag=tag + "c", name=tag + "c", align_bytes=64)
@@ -173,16 +187,13 @@ def tile_linearwdecoder_pb_kernel(tc, h, W3, b3, Wo, bo, out):
                 op=ADD,
             )
 
-        def mm2_and_bias(g):
+        def mm2(g):
             ac, as_ = h3c[g]
             wc, ws = woc[g]
-            if g % 2 == 0:
-                ots[g // 2] = res.tile([P, 2 * 2 * PD], F32, tag="ot", name="ot", bufs=3)
-            ot = ots[g // 2][:].rearrange("p (bb c) -> p bb c", bb=2)
-            ys = []
+            ys[g] = []
             for bb in range(2):
                 y = yp.tile([P, PD], F32, tag="y", name="y")
-                ys.append(y)
+                ys[g].append(y)
                 nc.tensor.matmul_mx(
                     out=y[:],
                     lhsT=ac[:, 128 * bb : 128 * bb + 128].bitcast(FP8X4),
@@ -192,14 +203,23 @@ def tile_linearwdecoder_pb_kernel(tc, h, W3, b3, Wo, bo, out):
                     start=True,
                     stop=True,
                 )
+
+        def add_bias(g):
+            if g % 2 == 0:
+                ots[g // 2] = res.tile([P, 2 * 2 * PD], F32, tag="ot", name="ot", bufs=3)
+            ot = ots[g // 2][:].rearrange("p (bb c) -> p bb c", bb=2)
             c0 = PD * (g % 2)
             for bb in range(2):
                 nc.vector.tensor_tensor(
                     out=ot[:, bb, c0 : c0 + PD].rearrange("p (q r) -> p q r", r=4),
-                    in0=ys[bb][:].rearrange("p (r q) -> p q r", r=4),
+                    in0=ys[g][bb][:].rearrange("p (r q) -> p q r", r=4),
                     in1=bo_bc[:, PD * g : PD * g + PD].rearrange("p (q r) -> p q r", r=4),
                     op=ADD,
                 )
+                if g == G - 1:
+                    nc.sync.dma_start(
+                        out=out_view[:, bb, PD * g : PD * g + PD], in_=ot[:, bb, c0 : c0 + PD]
+                    )
 
         def store(g0, g1):
             ot = ots[g0 // 2][:].rearrange("p (bb c) -> p bb c", bb=2)
@@ -210,33 +230,33 @@ def tile_linearwdecoder_pb_kernel(tc, h, W3, b3, Wo, bo, out):
 
         for g in range(LOOKAHEAD):
             load_w(g)
-        bank = tp.tile([P, 512], F32, tag="tp", name="b3bank")
-        nc.tensor.transpose(bank[:, 0:128], b3n[:].bitcast(F32), ident[:])
-        nc.vector.tensor_copy(out=b3c[:], in_=bank[:, 0 : 2 * G].bitcast(BF16))
         spread_bias(0)
 
-        for j in range(G + 3):
+        for j in range(G + 2):
             if j + LOOKAHEAD < G:
                 load_w(j + LOOKAHEAD)
             g = j - 3
             if 0 <= g < G - 2 and g % 2 == 1:
                 store(g - 1, g + 1)
-            if g >= G - 2:
+            if g == G - 2:
                 store(g, g + 1)
-            if 0 <= j - 2 < G:
+            if 0 <= j - 2 < G - 1:
                 residual(j - 2)
             if 0 <= j - 1 < G:
                 woc[j - 1] = quantise(wog[j - 1], PD, "wo")
-            if 0 <= j - 2 < G:
+            if 0 <= j - 2 < G - 1:
                 h3c[j - 2] = quantise(h3g[j - 2], B, "h3")
             if j < G:
-                transposes(j)
-                if j % 2 == 0 and j + 2 < G:
-                    spread_bias(j // 2 + 1)
+                transposes(j, HEAD_BIAS.get(j, ()))
                 w3c[j] = quantise(w3g[j], H, "w3")
                 hc[j] = quantise(hg[j], B, "h")
             if 0 <= j - 1 < G:
                 mm1(j - 1)
                 relu(j - 1)
             if 0 <= j - 2 < G:
-                mm2_and_bias(j - 2)
+                mm2(j - 2)
+            if j - 1 == G - 1:
+                residual(G - 1)
+                h3c[G - 1] = quantise(h3g[G - 1], B, "h3")
+            if 0 <= j - 2 < G:
+                add_bias(j - 2)

@@ -52,7 +52,7 @@ def tile_linearwdecoder_pb_kernel(tc, h, W3, b3, Wo, bo, out):
         b3c = const.tile([P, 4 * G], F32)
         bo_bc = const.tile([P, G * PD], BF16)
 
-        h_tiles = {}
+        h_words = {}
         w3n = {}
         won = {}
 
@@ -64,7 +64,7 @@ def tile_linearwdecoder_pb_kernel(tc, h, W3, b3, Wo, bo, out):
                 in_=h_view[:, :, g0 * H : g1 * H],
             )
             for g in range(g0, g1):
-                h_tiles[g] = (t, g1 - g0, g - g0)
+                h_words[g] = (t, [(bb * (g1 - g0) + g - g0) * 256 + 128 * u for bb in range(2) for u in range(2)])
 
         def load_w(g):
             a = wnat.tile([P, 4 * H], BF16, tag="w3n", name="w3n")
@@ -77,48 +77,47 @@ def tile_linearwdecoder_pb_kernel(tc, h, W3, b3, Wo, bo, out):
             nc.sync.dma_start(out=b[:], in_=wo_view[:, g])
             won[g] = b
 
-        w3g, wog, hg, h3g = {}, {}, {}, {}
+        banks = {}
+        grouped = {}
         w3c, woc, hc, h3c = {}, {}, {}, {}
-        xs, rs, ys, ots = {}, {}, {}, {}
+        h3g, xs, rs, ys, ots = {}, {}, {}, {}, {}
 
-        def flip(words, offsets, dst_words):
+        def flip(g, k):
+            if not 0 <= g < G:
+                return
+            if k < 2:
+                src, offsets = w3n[g], [512 * k + 128 * i for i in range(4)]
+            elif k == 2:
+                src, offsets = h_words[g]
+            else:
+                src, offsets = won[g], [512 * (k - 3) + 128 * i for i in range(4)]
             bank = tp.tile([P, 512], F32, tag="tp", name="bank")
+            banks[(g, k)] = bank
+            words = src[:].bitcast(F32)
             for i in range(4):
                 nc.tensor.transpose(
                     bank[:, 128 * i : 128 * i + 128], words[:, offsets[i] : offsets[i] + 128], ident[:]
                 )
-            nc.scalar.copy(
-                out=dst_words.rearrange("p (a q u) -> p a q u", a=2, u=2),
-                in_=bank[:].rearrange("p (a u q) -> p a q u", a=2, u=2),
-            )
 
-        def transposes(g, extra):
-            a = grp.tile([P, 4 * H], BF16, tag="w3g", name="w3g", align_bytes=64)
-            w3g[g] = a
-            src = w3n[g][:].bitcast(F32)
-            for half in range(2):
-                flip(src, [512 * half + 128 * i for i in range(4)], a[:].bitcast(F32)[:, 512 * half : 512 * half + 512])
-            if g == 0:
-                bias3_to_partitions()
-            if len(extra) > 0:
-                spread_bias(extra[0])
-            t, ng, gi = h_tiles[g]
-            c = grp.tile([P, 4 * B], BF16, tag="hg", name="hg", align_bytes=64, bufs=3)
-            hg[g] = c
-            flip(
-                t[:].bitcast(F32),
-                [(bb * ng + gi) * 256 + 128 * u for bb in range(2) for u in range(2)],
-                c[:].bitcast(F32),
+        def copy_out(g, k):
+            if not 0 <= g < G:
+                return
+            if k == 0:
+                grouped[(g, "w3")] = grp.tile([P, 4 * H], BF16, tag="w3g", name="w3g", align_bytes=64)
+            if k == 2:
+                grouped[(g, "h")] = grp.tile([P, 4 * B], BF16, tag="hg", name="hg", align_bytes=64, bufs=3)
+            if k == 3:
+                grouped[(g, "wo")] = grp.tile([P, 4 * PD], BF16, tag="wog", name="wog", align_bytes=64)
+            if k < 2:
+                dst = grouped[(g, "w3")][:].bitcast(F32)[:, 512 * k : 512 * k + 512]
+            elif k == 2:
+                dst = grouped[(g, "h")][:].bitcast(F32)
+            else:
+                dst = grouped[(g, "wo")][:].bitcast(F32)[:, 512 * (k - 3) : 512 * (k - 3) + 512]
+            nc.scalar.copy(
+                out=dst.rearrange("p (a q u) -> p a q u", a=2, u=2),
+                in_=banks[(g, k)][:].rearrange("p (a u q) -> p a q u", a=2, u=2),
             )
-            if len(extra) > 1:
-                spread_bias(extra[1])
-            b = grp.tile([P, 4 * PD], BF16, tag="wog", name="wog", align_bytes=64)
-            wog[g] = b
-            src = won[g][:].bitcast(F32)
-            for half in range(2):
-                flip(src, [512 * half + 128 * i for i in range(4)], b[:].bitcast(F32)[:, 512 * half : 512 * half + 512])
-            if len(extra) > 2:
-                spread_bias(extra[2])
 
         def bias3_to_partitions():
             bank = tp.tile([P, 512], F32, tag="tp", name="b3bank")
@@ -147,10 +146,10 @@ def tile_linearwdecoder_pb_kernel(tc, h, W3, b3, Wo, bo, out):
         def mm1(g):
             wc, ws = w3c[g]
             ac, as_ = hc[g]
-            banks = []
+            xs[g] = []
             for half in range(2):
                 x = xp.tile([P, 512], F32, tag="x", name="x")
-                banks.append(x)
+                xs[g].append(x)
                 for i in range(2):
                     t = 2 * half + i
                     nc.tensor.matmul_mx(
@@ -162,16 +161,14 @@ def tile_linearwdecoder_pb_kernel(tc, h, W3, b3, Wo, bo, out):
                         start=True,
                         stop=True,
                     )
-            xs[g] = banks
 
         def relu(g):
             r = res.tile([P, 4 * B], F32, tag="r", name="r")
             rs[g] = r
-            banks = xs[g]
             for t in range(4):
                 nc.scalar.activation(
                     out=r[:, 256 * t : 256 * t + 256],
-                    in_=banks[t // 2][:, 256 * (t % 2) : 256 * (t % 2) + 256],
+                    in_=xs[g][t // 2][:, 256 * (t % 2) : 256 * (t % 2) + 256],
                     func=RELU,
                     bias=b3c[:, 4 * g + t : 4 * g + t + 1],
                     scale=1.0,
@@ -183,7 +180,7 @@ def tile_linearwdecoder_pb_kernel(tc, h, W3, b3, Wo, bo, out):
             nc.vector.tensor_tensor(
                 out=s[:].rearrange("p (b t) -> p b t", t=4),
                 in0=rs[g][:].rearrange("p (t b) -> p b t", t=4),
-                in1=hg[g][:].rearrange("p (b t) -> p b t", t=4),
+                in1=grouped[(g, "h")][:].rearrange("p (b t) -> p b t", t=4),
                 op=ADD,
             )
 
@@ -231,6 +228,10 @@ def tile_linearwdecoder_pb_kernel(tc, h, W3, b3, Wo, bo, out):
         for g in range(LOOKAHEAD):
             load_w(g)
         spread_bias(0)
+        flip(0, 0)
+        flip(0, 1)
+        bias3_to_partitions()
+        flip(0, 2)
 
         for j in range(G + 2):
             if j + LOOKAHEAD < G:
@@ -243,15 +244,27 @@ def tile_linearwdecoder_pb_kernel(tc, h, W3, b3, Wo, bo, out):
             if 0 <= j - 2 < G - 1:
                 residual(j - 2)
             if 0 <= j - 1 < G:
-                woc[j - 1] = quantise(wog[j - 1], PD, "wo")
+                woc[j - 1] = quantise(grouped[(j - 1, "wo")], PD, "wo")
             if 0 <= j - 2 < G - 1:
                 h3c[j - 2] = quantise(h3g[j - 2], B, "h3")
-            if j < G:
-                transposes(j, HEAD_BIAS.get(j, ()))
-                w3c[j] = quantise(w3g[j], H, "w3")
-                hc[j] = quantise(hg[j], B, "h")
+            copy_out(j, 0)
+            copy_out(j, 1)
+            if j == 0:
+                flip(0, 3)
             if 0 <= j - 1 < G:
                 mm1(j - 1)
+            copy_out(j, 2)
+            copy_out(j, 3)
+            flip(j, 4)
+            copy_out(j, 4)
+            if j < G:
+                w3c[j] = quantise(grouped[(j, "w3")], H, "w3")
+                hc[j] = quantise(grouped[(j, "h")], B, "h")
+            for c in HEAD_BIAS.get(j, ()):
+                spread_bias(c)
+            flip(j + 1, 0)
+            flip(j + 1, 1)
+            if 0 <= j - 1 < G:
                 relu(j - 1)
             if 0 <= j - 2 < G:
                 mm2(j - 2)
@@ -260,3 +273,5 @@ def tile_linearwdecoder_pb_kernel(tc, h, W3, b3, Wo, bo, out):
                 h3c[G - 1] = quantise(h3g[G - 1], B, "h3")
             if 0 <= j - 2 < G:
                 add_bias(j - 2)
+            flip(j + 1, 2)
+            flip(j + 1, 3)

@@ -105,7 +105,7 @@ def tile_linearwdecoder_pb_kernel(tc, h, W3, b3, Wo, bo, out):
             if k == 0:
                 grouped[(g, "w3")] = grp.tile([P, 4 * H], BF16, tag="w3g", name="w3g", align_bytes=64)
             if k == 2:
-                grouped[(g, "h")] = grp.tile([P, 4 * B], BF16, tag="hg", name="hg", align_bytes=64, bufs=3)
+                grouped[(g, "h")] = grp.tile([P, 4 * B], BF16, tag="hg", name="hg", align_bytes=64, bufs=4)
             if k == 3:
                 grouped[(g, "wo")] = grp.tile([P, 4 * PD], BF16, tag="wog", name="wog", align_bytes=64)
             if k < 2:
@@ -177,12 +177,14 @@ def tile_linearwdecoder_pb_kernel(tc, h, W3, b3, Wo, bo, out):
         def residual(g):
             s = grp.tile([P, 4 * B], BF16, tag="h3g", name="h3g", align_bytes=64)
             h3g[g] = s
-            nc.vector.tensor_tensor(
-                out=s[:].rearrange("p (b t) -> p b t", t=4),
-                in0=rs[g][:].rearrange("p (t b) -> p b t", t=4),
-                in1=grouped[(g, "h")][:].rearrange("p (b t) -> p b t", t=4),
-                op=ADD,
-            )
+            dst = s[:].rearrange("p (b t) -> p b t", t=4)
+            relu_part = rs[g][:].rearrange("p (t b) -> p b t", t=4)
+            skip_part = grouped[(g, "h")][:].rearrange("p (b t) -> p b t", t=4)
+            for bb in range(2):
+                cols = slice(P * bb, P * bb + P)
+                nc.gpsimd.tensor_tensor(
+                    out=dst[:, cols, :], in0=relu_part[:, cols, :], in1=skip_part[:, cols, :], op=ADD
+                )
 
         def mm2(g):
             ac, as_ = h3c[g]
@@ -233,26 +235,24 @@ def tile_linearwdecoder_pb_kernel(tc, h, W3, b3, Wo, bo, out):
         bias3_to_partitions()
         flip(0, 2)
 
-        for j in range(G + 2):
+        for j in range(G + 3):
             if j + LOOKAHEAD < G:
                 load_w(j + LOOKAHEAD)
-            g = j - 3
-            if 0 <= g < G - 2 and g % 2 == 1:
-                store(g - 1, g + 1)
-            if g == G - 2:
-                store(g, g + 1)
-            if 0 <= j - 2 < G - 1:
+            if 0 <= j - 2 < G:
                 residual(j - 2)
+            g = j - 3
+            if 0 <= g < G:
+                add_bias(g)
+                if g < G - 2 and g % 2 == 1:
+                    store(g - 1, g + 1)
+                if g == G - 2:
+                    store(g, g + 1)
             if 0 <= j - 1 < G:
                 woc[j - 1] = quantise(grouped[(j - 1, "wo")], PD, "wo")
-            if 0 <= j - 2 < G - 1:
-                h3c[j - 2] = quantise(h3g[j - 2], B, "h3")
             copy_out(j, 0)
             copy_out(j, 1)
             if j == 0:
                 flip(0, 3)
-            if 0 <= j - 1 < G:
-                mm1(j - 1)
             copy_out(j, 2)
             copy_out(j, 3)
             flip(j, 4)
@@ -263,15 +263,12 @@ def tile_linearwdecoder_pb_kernel(tc, h, W3, b3, Wo, bo, out):
             for c in HEAD_BIAS.get(j, ()):
                 spread_bias(c)
             flip(j + 1, 0)
-            flip(j + 1, 1)
             if 0 <= j - 1 < G:
+                mm1(j - 1)
                 relu(j - 1)
-            if 0 <= j - 2 < G:
-                mm2(j - 2)
-            if j - 1 == G - 1:
-                residual(G - 1)
-                h3c[G - 1] = quantise(h3g[G - 1], B, "h3")
-            if 0 <= j - 2 < G:
-                add_bias(j - 2)
+            flip(j + 1, 1)
             flip(j + 1, 2)
             flip(j + 1, 3)
+            if 0 <= j - 2 < G:
+                h3c[j - 2] = quantise(h3g[j - 2], B, "h3")
+                mm2(j - 2)

@@ -17,7 +17,8 @@ FLOPS = 2 * B * G * H * (H + PD)
 
 W_BUFS = 8
 LOOKAHEAD = W_BUFS - 1
-HEAD_BIAS = {0: (1, 2, 3), 1: (4, 5, 6), 2: (7,)}
+HEAD_BIAS = {0: (1, 2, 3), 1: (4, 5, 6, 7)}
+SKIP = 5
 H_CHUNKS = ((0, 2), (2, 4), (4, 8), (8, 12), (12, 16))
 
 
@@ -29,7 +30,8 @@ def tile_linearwdecoder_pb_kernel(tc, h, W3, b3, Wo, bo, out):
         grp = ctx.enter_context(tc.tile_pool(name="grp", bufs=2))
         cod = ctx.enter_context(tc.tile_pool(name="cod", bufs=2))
         res = ctx.enter_context(tc.tile_pool(name="res", bufs=2))
-        tp = ctx.enter_context(tc.psum_pool(name="tp", bufs=4))
+        tp = ctx.enter_context(tc.psum_pool(name="tp", bufs=3))
+        sp = ctx.enter_context(tc.psum_pool(name="sp", bufs=1))
         xp = ctx.enter_context(tc.psum_pool(name="xp", bufs=2))
         yp = ctx.enter_context(tc.psum_pool(name="yp", bufs=2))
         ctx.enter_context(tc.manual_schedule())
@@ -87,11 +89,14 @@ def tile_linearwdecoder_pb_kernel(tc, h, W3, b3, Wo, bo, out):
                 return
             if k < 2:
                 src, offsets = w3n[g], [512 * k + 128 * i for i in range(4)]
-            elif k == 2:
+            elif k == 2 or k == SKIP:
                 src, offsets = h_words[g]
             else:
                 src, offsets = won[g], [512 * (k - 3) + 128 * i for i in range(4)]
-            bank = tp.tile([P, 512], F32, tag="tp", name="bank")
+            if k == SKIP:
+                bank = sp.tile([P, 512], F32, tag="skip", name="skip")
+            else:
+                bank = tp.tile([P, 512], F32, tag="tp", name="bank")
             banks[(g, k)] = bank
             words = src[:].bitcast(F32)
             for i in range(4):
@@ -105,7 +110,7 @@ def tile_linearwdecoder_pb_kernel(tc, h, W3, b3, Wo, bo, out):
             if k == 0:
                 grouped[(g, "w3")] = grp.tile([P, 4 * H], BF16, tag="w3g", name="w3g", align_bytes=64)
             if k == 2:
-                grouped[(g, "h")] = grp.tile([P, 4 * B], BF16, tag="hg", name="hg", align_bytes=64, bufs=4)
+                grouped[(g, "h")] = grp.tile([P, 4 * B], BF16, tag="hg", name="hg", align_bytes=64)
             if k == 3:
                 grouped[(g, "wo")] = grp.tile([P, 4 * PD], BF16, tag="wog", name="wog", align_bytes=64)
             if k < 2:
@@ -120,12 +125,12 @@ def tile_linearwdecoder_pb_kernel(tc, h, W3, b3, Wo, bo, out):
             )
 
         def bias3_to_partitions():
-            bank = tp.tile([P, 512], F32, tag="tp", name="b3bank")
+            bank = sp.tile([P, 512], F32, tag="skip", name="b3bank")
             nc.tensor.transpose(bank[:, 0:128], b3n[:].bitcast(F32), ident[:])
             nc.vector.tensor_copy(out=b3c[:], in_=bank[:, 0 : 2 * G].bitcast(BF16))
 
         def spread_bias(c):
-            bank = tp.tile([P, 1024], BF16, tag="tp", name="bbank")
+            bank = yp.tile([P, 1024], BF16, tag="y", name="bbank")
             for i in range(2):
                 g = 2 * c + i
                 nc.tensor.matmul(
@@ -177,14 +182,11 @@ def tile_linearwdecoder_pb_kernel(tc, h, W3, b3, Wo, bo, out):
         def residual(g):
             s = grp.tile([P, 4 * B], BF16, tag="h3g", name="h3g", align_bytes=64)
             h3g[g] = s
-            dst = s[:].rearrange("p (b t) -> p b t", t=4)
-            relu_part = rs[g][:].rearrange("p (t b) -> p b t", t=4)
-            skip_part = grouped[(g, "h")][:].rearrange("p (b t) -> p b t", t=4)
+            dst = s[:].rearrange("p (bb m u e) -> p bb m u e", bb=2, u=2, e=2)
+            relu_part = rs[g][:].rearrange("p (u e bb m) -> p bb m u e", u=2, e=2, bb=2)
+            skip_part = banks[(g, SKIP)][:].bitcast(BF16).rearrange("p (bb u m e) -> p bb m u e", bb=2, u=2, e=2)
             for bb in range(2):
-                cols = slice(P * bb, P * bb + P)
-                nc.gpsimd.tensor_tensor(
-                    out=dst[:, cols, :], in0=relu_part[:, cols, :], in1=skip_part[:, cols, :], op=ADD
-                )
+                nc.vector.tensor_tensor(out=dst[:, bb], in0=relu_part[:, bb], in1=skip_part[:, bb], op=ADD)
 
         def mm2(g):
             ac, as_ = h3c[g]
@@ -232,43 +234,48 @@ def tile_linearwdecoder_pb_kernel(tc, h, W3, b3, Wo, bo, out):
         spread_bias(0)
         flip(0, 0)
         flip(0, 1)
-        bias3_to_partitions()
         flip(0, 2)
 
-        for j in range(G + 3):
+        for j in range(G + 2):
             if j + LOOKAHEAD < G:
                 load_w(j + LOOKAHEAD)
-            if 0 <= j - 2 < G:
-                residual(j - 2)
             g = j - 3
-            if 0 <= g < G:
-                add_bias(g)
-                if g < G - 2 and g % 2 == 1:
-                    store(g - 1, g + 1)
-                if g == G - 2:
-                    store(g, g + 1)
+            if 0 <= g < G - 2 and g % 2 == 1:
+                store(g - 1, g + 1)
+            if g == G - 2:
+                store(g, g + 1)
+            if 0 <= j - 2 < G - 1:
+                residual(j - 2)
             if 0 <= j - 1 < G:
                 woc[j - 1] = quantise(grouped[(j - 1, "wo")], PD, "wo")
+            if 0 <= j - 2 < G - 1:
+                h3c[j - 2] = quantise(h3g[j - 2], B, "h3")
             copy_out(j, 0)
+            if 0 <= j - 1 < G:
+                mm1(j - 1)
+            flip(j, 3)
             copy_out(j, 1)
-            if j == 0:
-                flip(0, 3)
-            copy_out(j, 2)
-            copy_out(j, 3)
             flip(j, 4)
-            copy_out(j, 4)
+            copy_out(j, 2)
+            flip(j + 1, 0)
+            copy_out(j, 3)
             if j < G:
                 w3c[j] = quantise(grouped[(j, "w3")], H, "w3")
                 hc[j] = quantise(grouped[(j, "h")], B, "h")
             for c in HEAD_BIAS.get(j, ()):
                 spread_bias(c)
-            flip(j + 1, 0)
-            if 0 <= j - 1 < G:
-                mm1(j - 1)
-                relu(j - 1)
-            flip(j + 1, 1)
-            flip(j + 1, 2)
-            flip(j + 1, 3)
+            if j == 0:
+                bias3_to_partitions()
             if 0 <= j - 2 < G:
-                h3c[j - 2] = quantise(h3g[j - 2], B, "h3")
                 mm2(j - 2)
+            flip(j + 1, 1)
+            copy_out(j, 4)
+            flip(j + 1, 2)
+            if 0 <= j - 1 < G:
+                relu(j - 1)
+                flip(j - 1, SKIP)
+            if j - 1 == G - 1:
+                residual(G - 1)
+                h3c[G - 1] = quantise(h3g[G - 1], B, "h3")
+            if 0 <= j - 2 < G:
+                add_bias(j - 2)

@@ -17,8 +17,7 @@ FLOPS = 2 * B * G * H * (H + PD)
 
 W_BUFS = 8
 LOOKAHEAD = W_BUFS - 1
-HEAD_BIAS = {0: (1, 2, 3), 1: (4, 5, 6, 7)}
-SKIP = 5
+HEAD_BIAS = {0: (1, 2, 3), 1: (4, 5, 6), 2: (7,)}
 H_CHUNKS = ((0, 2), (2, 4), (4, 8), (8, 12), (12, 16))
 
 
@@ -30,8 +29,7 @@ def tile_linearwdecoder_pb_kernel(tc, h, W3, b3, Wo, bo, out):
         grp = ctx.enter_context(tc.tile_pool(name="grp", bufs=2))
         cod = ctx.enter_context(tc.tile_pool(name="cod", bufs=2))
         res = ctx.enter_context(tc.tile_pool(name="res", bufs=2))
-        tp = ctx.enter_context(tc.psum_pool(name="tp", bufs=3))
-        sp = ctx.enter_context(tc.psum_pool(name="sp", bufs=1))
+        tp = ctx.enter_context(tc.psum_pool(name="tp", bufs=4))
         xp = ctx.enter_context(tc.psum_pool(name="xp", bufs=2))
         yp = ctx.enter_context(tc.psum_pool(name="yp", bufs=2))
         ctx.enter_context(tc.manual_schedule())
@@ -84,20 +82,19 @@ def tile_linearwdecoder_pb_kernel(tc, h, W3, b3, Wo, bo, out):
         w3c, woc, hc, h3c = {}, {}, {}, {}
         h3g, xs, rs, ys, ots = {}, {}, {}, {}, {}
 
-        def flip(g, k):
+        def flip(g, k, repeat=None):
             if not 0 <= g < G:
                 return
             if k < 2:
                 src, offsets = w3n[g], [512 * k + 128 * i for i in range(4)]
-            elif k == 2 or k == SKIP:
+            elif k == 2:
                 src, offsets = h_words[g]
             else:
                 src, offsets = won[g], [512 * (k - 3) + 128 * i for i in range(4)]
-            if k == SKIP:
-                bank = sp.tile([P, 512], F32, tag="skip", name="skip")
-            else:
-                bank = tp.tile([P, 512], F32, tag="tp", name="bank")
+            bank = tp.tile([P, 512], F32, tag="tp", name="bank")
             banks[(g, k)] = bank
+            if repeat is not None:
+                repeat(bank)
             words = src[:].bitcast(F32)
             for i in range(4):
                 nc.tensor.transpose(
@@ -110,7 +107,7 @@ def tile_linearwdecoder_pb_kernel(tc, h, W3, b3, Wo, bo, out):
             if k == 0:
                 grouped[(g, "w3")] = grp.tile([P, 4 * H], BF16, tag="w3g", name="w3g", align_bytes=64)
             if k == 2:
-                grouped[(g, "h")] = grp.tile([P, 4 * B], BF16, tag="hg", name="hg", align_bytes=64)
+                grouped[(g, "h")] = grp.tile([P, 4 * B], BF16, tag="hg", name="hg", align_bytes=64, bufs=3)
             if k == 3:
                 grouped[(g, "wo")] = grp.tile([P, 4 * PD], BF16, tag="wog", name="wog", align_bytes=64)
             if k < 2:
@@ -125,12 +122,12 @@ def tile_linearwdecoder_pb_kernel(tc, h, W3, b3, Wo, bo, out):
             )
 
         def bias3_to_partitions():
-            bank = sp.tile([P, 512], F32, tag="skip", name="b3bank")
+            bank = tp.tile([P, 512], F32, tag="tp", name="b3bank")
             nc.tensor.transpose(bank[:, 0:128], b3n[:].bitcast(F32), ident[:])
             nc.vector.tensor_copy(out=b3c[:], in_=bank[:, 0 : 2 * G].bitcast(BF16))
 
         def spread_bias(c):
-            bank = yp.tile([P, 1024], BF16, tag="y", name="bbank")
+            bank = tp.tile([P, 1024], BF16, tag="tp", name="bbank")
             for i in range(2):
                 g = 2 * c + i
                 nc.tensor.matmul(
@@ -167,6 +164,41 @@ def tile_linearwdecoder_pb_kernel(tc, h, W3, b3, Wo, bo, out):
                         stop=True,
                     )
 
+        def repeat_mm1(g):
+            wc, ws = w3c[g]
+            ac, as_ = hc[g]
+
+            def passes(bank):
+                for i in range(2):
+                    nc.tensor.matmul_mx(
+                        out=bank[:, 256 * i : 256 * i + 256],
+                        lhsT=wc[:, 128 * i : 128 * i + 128].bitcast(FP8X4),
+                        lhsT_scale=ws[:, 128 * i : 128 * i + 128],
+                        rhs=ac[:].bitcast(FP8X4),
+                        rhs_scale=as_[:],
+                        start=True,
+                        stop=True,
+                    )
+
+            return passes
+
+        def repeat_mm2(g):
+            ac, as_ = h3c[g]
+            wc, ws = woc[g]
+
+            def passes(bank):
+                nc.tensor.matmul_mx(
+                    out=bank[:],
+                    lhsT=ac[:, 0:128].bitcast(FP8X4),
+                    lhsT_scale=as_[:, 0:128],
+                    rhs=wc[:].bitcast(FP8X4),
+                    rhs_scale=ws[:],
+                    start=True,
+                    stop=True,
+                )
+
+            return passes
+
         def relu(g):
             r = res.tile([P, 4 * B], F32, tag="r", name="r")
             rs[g] = r
@@ -182,11 +214,12 @@ def tile_linearwdecoder_pb_kernel(tc, h, W3, b3, Wo, bo, out):
         def residual(g):
             s = grp.tile([P, 4 * B], BF16, tag="h3g", name="h3g", align_bytes=64)
             h3g[g] = s
-            dst = s[:].rearrange("p (bb m u e) -> p bb m u e", bb=2, u=2, e=2)
-            relu_part = rs[g][:].rearrange("p (u e bb m) -> p bb m u e", u=2, e=2, bb=2)
-            skip_part = banks[(g, SKIP)][:].bitcast(BF16).rearrange("p (bb u m e) -> p bb m u e", bb=2, u=2, e=2)
-            for bb in range(2):
-                nc.vector.tensor_tensor(out=dst[:, bb], in0=relu_part[:, bb], in1=skip_part[:, bb], op=ADD)
+            nc.vector.tensor_tensor(
+                out=s[:].rearrange("p (b t) -> p b t", t=4),
+                in0=rs[g][:].rearrange("p (t b) -> p b t", t=4),
+                in1=grouped[(g, "h")][:].rearrange("p (b t) -> p b t", t=4),
+                op=ADD,
+            )
 
         def mm2(g):
             ac, as_ = h3c[g]
@@ -234,6 +267,7 @@ def tile_linearwdecoder_pb_kernel(tc, h, W3, b3, Wo, bo, out):
         spread_bias(0)
         flip(0, 0)
         flip(0, 1)
+        bias3_to_partitions()
         flip(0, 2)
 
         for j in range(G + 2):
@@ -251,31 +285,30 @@ def tile_linearwdecoder_pb_kernel(tc, h, W3, b3, Wo, bo, out):
             if 0 <= j - 2 < G - 1:
                 h3c[j - 2] = quantise(h3g[j - 2], B, "h3")
             copy_out(j, 0)
+            copy_out(j, 1)
+            if j == 0:
+                flip(0, 3)
             if 0 <= j - 1 < G:
                 mm1(j - 1)
-            flip(j, 3)
-            copy_out(j, 1)
-            flip(j, 4)
             copy_out(j, 2)
-            flip(j + 1, 0)
             copy_out(j, 3)
+            flip(j, 4, repeat_mm1(j - 1) if 0 <= j - 1 < G else None)
+            copy_out(j, 4)
             if j < G:
                 w3c[j] = quantise(grouped[(j, "w3")], H, "w3")
                 hc[j] = quantise(grouped[(j, "h")], B, "h")
             for c in HEAD_BIAS.get(j, ()):
                 spread_bias(c)
-            if j == 0:
-                bias3_to_partitions()
-            if 0 <= j - 2 < G:
-                mm2(j - 2)
+            flip(j + 1, 0)
             flip(j + 1, 1)
-            copy_out(j, 4)
-            flip(j + 1, 2)
             if 0 <= j - 1 < G:
                 relu(j - 1)
-                flip(j - 1, SKIP)
+            if 0 <= j - 2 < G:
+                mm2(j - 2)
             if j - 1 == G - 1:
                 residual(G - 1)
                 h3c[G - 1] = quantise(h3g[G - 1], B, "h3")
             if 0 <= j - 2 < G:
                 add_bias(j - 2)
+            flip(j + 1, 2, repeat_mm2(j - 2) if 0 <= j - 2 < G else None)
+            flip(j + 1, 3)

@@ -82,7 +82,7 @@ def tile_linearwdecoder_pb_kernel(tc, h, W3, b3, Wo, bo, out):
         w3c, woc, hc, h3c = {}, {}, {}, {}
         h3g, xs, rs, ys, ots = {}, {}, {}, {}, {}
 
-        def flip(g, k, repeat=None):
+        def flip(g, k):
             if not 0 <= g < G:
                 return
             if k < 2:
@@ -93,8 +93,6 @@ def tile_linearwdecoder_pb_kernel(tc, h, W3, b3, Wo, bo, out):
                 src, offsets = won[g], [512 * (k - 3) + 128 * i for i in range(4)]
             bank = tp.tile([P, 512], F32, tag="tp", name="bank")
             banks[(g, k)] = bank
-            if repeat is not None:
-                repeat(bank)
             words = src[:].bitcast(F32)
             for i in range(4):
                 nc.tensor.transpose(
@@ -164,41 +162,6 @@ def tile_linearwdecoder_pb_kernel(tc, h, W3, b3, Wo, bo, out):
                         stop=True,
                     )
 
-        def repeat_mm1(g):
-            wc, ws = w3c[g]
-            ac, as_ = hc[g]
-
-            def passes(bank):
-                for i in range(2):
-                    nc.tensor.matmul_mx(
-                        out=bank[:, 256 * i : 256 * i + 256],
-                        lhsT=wc[:, 128 * i : 128 * i + 128].bitcast(FP8X4),
-                        lhsT_scale=ws[:, 128 * i : 128 * i + 128],
-                        rhs=ac[:].bitcast(FP8X4),
-                        rhs_scale=as_[:],
-                        start=True,
-                        stop=True,
-                    )
-
-            return passes
-
-        def repeat_mm2(g):
-            ac, as_ = h3c[g]
-            wc, ws = woc[g]
-
-            def passes(bank):
-                nc.tensor.matmul_mx(
-                    out=bank[:],
-                    lhsT=ac[:, 0:128].bitcast(FP8X4),
-                    lhsT_scale=as_[:, 0:128],
-                    rhs=wc[:].bitcast(FP8X4),
-                    rhs_scale=ws[:],
-                    start=True,
-                    stop=True,
-                )
-
-            return passes
-
         def relu(g):
             r = res.tile([P, 4 * B], F32, tag="r", name="r")
             rs[g] = r
@@ -215,9 +178,9 @@ def tile_linearwdecoder_pb_kernel(tc, h, W3, b3, Wo, bo, out):
             s = grp.tile([P, 4 * B], BF16, tag="h3g", name="h3g", align_bytes=64)
             h3g[g] = s
             nc.vector.tensor_tensor(
-                out=s[:].rearrange("p (b t) -> p b t", t=4),
-                in0=rs[g][:].rearrange("p (t b) -> p b t", t=4),
-                in1=grouped[(g, "h")][:].rearrange("p (b t) -> p b t", t=4),
+                out=s[:].rearrange("p (c i t) -> p c t i", i=4, t=4),
+                in0=rs[g][:].rearrange("p (t c i) -> p c t i", t=4, i=4),
+                in1=grouped[(g, "h")][:].rearrange("p (c i t) -> p c t i", i=4, t=4),
                 op=ADD,
             )
 
@@ -292,7 +255,7 @@ def tile_linearwdecoder_pb_kernel(tc, h, W3, b3, Wo, bo, out):
                 mm1(j - 1)
             copy_out(j, 2)
             copy_out(j, 3)
-            flip(j, 4, repeat_mm1(j - 1) if 0 <= j - 1 < G else None)
+            flip(j, 4)
             copy_out(j, 4)
             if j < G:
                 w3c[j] = quantise(grouped[(j, "w3")], H, "w3")
@@ -310,5 +273,5 @@ def tile_linearwdecoder_pb_kernel(tc, h, W3, b3, Wo, bo, out):
                 h3c[G - 1] = quantise(h3g[G - 1], B, "h3")
             if 0 <= j - 2 < G:
                 add_bias(j - 2)
-            flip(j + 1, 2, repeat_mm2(j - 2) if 0 <= j - 2 < G else None)
+            flip(j + 1, 2)
             flip(j + 1, 3)

@@ -17,7 +17,7 @@ FLOPS = 2 * B * G * H * (H + PD)
 
 W_BUFS = 8
 LOOKAHEAD = W_BUFS - 1
-HEAD_BIAS = {0: (1, 2, 3), 1: (4, 5, 6), 2: (7,)}
+HEAD_BIAS = {0: (1, 2), 1: (3, 4, 5), 2: (6, 7)}
 H_CHUNKS = ((0, 2), (2, 4), (4, 8), (8, 12), (12, 16))
 
 
@@ -125,7 +125,7 @@ def tile_linearwdecoder_pb_kernel(tc, h, W3, b3, Wo, bo, out):
             nc.vector.tensor_copy(out=b3c[:], in_=bank[:, 0 : 2 * G].bitcast(BF16))
 
         def spread_bias(c):
-            bank = tp.tile([P, 1024], BF16, tag="tp", name="bbank")
+            bank = yp.tile([P, 1024], BF16, tag="y", name="bbank")
             for i in range(2):
                 g = 2 * c + i
                 nc.tensor.matmul(
@@ -137,9 +137,9 @@ def tile_linearwdecoder_pb_kernel(tc, h, W3, b3, Wo, bo, out):
                 )
             nc.vector.tensor_copy(out=bo_bc[:, 1024 * c : 1024 * c + 1024], in_=bank[:])
 
-        def quantise(src, width, tag):
-            codes = cod.tile([P, width], U32, tag=tag + "c", name=tag + "c", align_bytes=64)
-            scales = cod.tile([P, width], U8, tag=tag + "s", name=tag + "s", align_bytes=64)
+        def quantise(src, width, tag, bufs=2):
+            codes = cod.tile([P, width], U32, tag=tag + "c", name=tag + "c", align_bytes=64, bufs=bufs)
+            scales = cod.tile([P, width], U8, tag=tag + "s", name=tag + "s", align_bytes=64, bufs=bufs)
             nc.vector.quantize_mx(out=codes[:].bitcast(FP8X4), scales=scales[:], in_=src[:])
             return codes, scales
 
@@ -233,19 +233,14 @@ def tile_linearwdecoder_pb_kernel(tc, h, W3, b3, Wo, bo, out):
         bias3_to_partitions()
         flip(0, 2)
 
-        for j in range(G + 2):
+        for j in range(G + 3):
             if j + LOOKAHEAD < G:
                 load_w(j + LOOKAHEAD)
-            g = j - 3
-            if 0 <= g < G - 2 and g % 2 == 1:
-                store(g - 1, g + 1)
-            if g == G - 2:
-                store(g, g + 1)
-            if 0 <= j - 2 < G - 1:
+            if 0 <= j - 2 < G:
                 residual(j - 2)
             if 0 <= j - 1 < G:
-                woc[j - 1] = quantise(grouped[(j - 1, "wo")], PD, "wo")
-            if 0 <= j - 2 < G - 1:
+                woc[j - 1] = quantise(grouped[(j - 1, "wo")], PD, "wo", bufs=3)
+            if 0 <= j - 2 < G:
                 h3c[j - 2] = quantise(h3g[j - 2], B, "h3")
             copy_out(j, 0)
             copy_out(j, 1)
@@ -260,18 +255,19 @@ def tile_linearwdecoder_pb_kernel(tc, h, W3, b3, Wo, bo, out):
             if j < G:
                 w3c[j] = quantise(grouped[(j, "w3")], H, "w3")
                 hc[j] = quantise(grouped[(j, "h")], B, "h")
-            for c in HEAD_BIAS.get(j, ()):
-                spread_bias(c)
             flip(j + 1, 0)
             flip(j + 1, 1)
             if 0 <= j - 1 < G:
                 relu(j - 1)
-            if 0 <= j - 2 < G:
-                mm2(j - 2)
-            if j - 1 == G - 1:
-                residual(G - 1)
-                h3c[G - 1] = quantise(h3g[G - 1], B, "h3")
-            if 0 <= j - 2 < G:
-                add_bias(j - 2)
+            g = j - 3
+            if 0 <= g < G:
+                mm2(g)
+                add_bias(g)
+                if g < G - 2 and g % 2 == 1:
+                    store(g - 1, g + 1)
+                if g == G - 2:
+                    store(g, g + 1)
             flip(j + 1, 2)
             flip(j + 1, 3)
+            for c in HEAD_BIAS.get(j, ()):
+                spread_bias(c)

from contextlib import ExitStack

import concourse.mybir as mybir
from concourse.masks import make_identity

F32 = mybir.dt.float32
BF16 = mybir.dt.bfloat16
U32 = mybir.dt.uint32
U8 = mybir.dt.uint8
FP8X4 = mybir.dt.float8_e4m3fn_x4
ADD = mybir.AluOpType.add
RELU = mybir.ActivationFunctionType.Relu

P = 128
B, G, H, PD = 256, 16, 512, 512
FLOPS = 2 * B * G * H * (H + PD)

W_BUFS = 8
LOOKAHEAD = W_BUFS - 1
HEAD_BIAS = {0: (1, 2), 1: (3, 4, 5), 2: (6, 7)}
H_CHUNKS = ((0, 2), (2, 4), (4, 8), (8, 12), (12, 16))


def tile_linearwdecoder_pb_kernel(tc, h, W3, b3, Wo, bo, out):
    nc = tc.nc
    with ExitStack() as ctx:
        const = ctx.enter_context(tc.tile_pool(name="const", bufs=1))
        wnat = ctx.enter_context(tc.tile_pool(name="wnat", bufs=W_BUFS))
        grp = ctx.enter_context(tc.tile_pool(name="grp", bufs=2))
        cod = ctx.enter_context(tc.tile_pool(name="cod", bufs=2))
        res = ctx.enter_context(tc.tile_pool(name="res", bufs=2))
        tp = ctx.enter_context(tc.psum_pool(name="tp", bufs=4))
        xp = ctx.enter_context(tc.psum_pool(name="xp", bufs=2))
        yp = ctx.enter_context(tc.psum_pool(name="yp", bufs=2))
        ctx.enter_context(tc.manual_schedule())

        w3_view = W3.rearrange("g (u q e) k -> q g u (e k)", u=2, q=P, e=2)
        wo_view = Wo.rearrange("g (q r) k -> q g (r k)", r=4)
        h_view = h.rearrange("(bb m) g k -> m bb (g k)", m=P)
        out_view = out.rearrange("(bb m) c -> m bb c", m=P)

        b3n = const.tile([P, 256], BF16)
        bo16 = const.tile([P, PD], BF16)
        nc.vector.memset(b3n[:], 0.0)
        nc.vector.memset(bo16[:], 0.0)
        nc.sync.dma_start(out=bo16[0:G, :], in_=bo)
        nc.sync.dma_start(out=b3n[0:32, :], in_=b3.rearrange("g (u w) -> (g u) w", u=2))
        ident = const.tile([P, P], F32)
        make_identity(nc, ident[:])
        identb = const.tile([P, P], BF16)
        make_identity(nc, identb[:])
        b3c = const.tile([P, 4 * G], F32)
        bo_bc = const.tile([P, G * PD], BF16)

        h_words = {}
        w3n = {}
        won = {}

        def load_h(c):
            g0, g1 = H_CHUNKS[c]
            t = const.tile([P, 2 * (g1 - g0) * H], BF16, name="hnat%d" % c)
            nc.sync.dma_start(
                out=t[:].rearrange("p (bb x) -> p bb x", bb=2),
                in_=h_view[:, :, g0 * H : g1 * H],
            )
            for g in range(g0, g1):
                h_words[g] = (t, [(bb * (g1 - g0) + g - g0) * 256 + 128 * u for bb in range(2) for u in range(2)])

        def load_w(g):
            a = wnat.tile([P, 4 * H], BF16, tag="w3n", name="w3n")
            nc.sync.dma_start(out=a[:].rearrange("p (u x) -> p u x", u=2), in_=w3_view[:, g])
            w3n[g] = a
            for c in range(len(H_CHUNKS)):
                if H_CHUNKS[c][0] == g:
                    load_h(c)
            b = wnat.tile([P, 4 * H], BF16, tag="won", name="won")
            nc.sync.dma_start(out=b[:], in_=wo_view[:, g])
            won[g] = b

        banks = {}
        grouped = {}
        w3c, woc, hc, h3c = {}, {}, {}, {}
        h3g, xs, rs, ys, ots = {}, {}, {}, {}, {}

        def flip(g, k):
            if not 0 <= g < G:
                return
            if k < 2:
                src, offsets = w3n[g], [512 * k + 128 * i for i in range(4)]
            elif k == 2:
                src, offsets = h_words[g]
            else:
                src, offsets = won[g], [512 * (k - 3) + 128 * i for i in range(4)]
            bank = tp.tile([P, 512], F32, tag="tp", name="bank")
            banks[(g, k)] = bank
            words = src[:].bitcast(F32)
            for i in range(4):
                nc.tensor.transpose(
                    bank[:, 128 * i : 128 * i + 128], words[:, offsets[i] : offsets[i] + 128], ident[:]
                )

        def copy_out(g, k):
            if not 0 <= g < G:
                return
            if k == 0:
                grouped[(g, "w3")] = grp.tile([P, 4 * H], BF16, tag="w3g", name="w3g", align_bytes=64)
            if k == 2:
                grouped[(g, "h")] = grp.tile([P, 4 * B], BF16, tag="hg", name="hg", align_bytes=64, bufs=3)
            if k == 3:
                grouped[(g, "wo")] = grp.tile([P, 4 * PD], BF16, tag="wog", name="wog", align_bytes=64)
            if k < 2:
                dst = grouped[(g, "w3")][:].bitcast(F32)[:, 512 * k : 512 * k + 512]
            elif k == 2:
                dst = grouped[(g, "h")][:].bitcast(F32)
            else:
                dst = grouped[(g, "wo")][:].bitcast(F32)[:, 512 * (k - 3) : 512 * (k - 3) + 512]
            nc.scalar.copy(
                out=dst.rearrange("p (a q u) -> p a q u", a=2, u=2),
                in_=banks[(g, k)][:].rearrange("p (a u q) -> p a q u", a=2, u=2),
            )

        def bias3_to_partitions():
            bank = tp.tile([P, 512], F32, tag="tp", name="b3bank")
            nc.tensor.transpose(bank[:, 0:128], b3n[:].bitcast(F32), ident[:])
            nc.vector.tensor_copy(out=b3c[:], in_=bank[:, 0 : 2 * G].bitcast(BF16))

        def spread_bias(c):
            bank = yp.tile([P, 1024], BF16, tag="y", name="bbank")
            for i in range(2):
                g = 2 * c + i
                nc.tensor.matmul(
                    bank[:, 512 * i : 512 * i + 512],
                    lhsT=identb[:, g : g + 1].to_broadcast([P, P]),
                    rhs=bo16[:],
                    start=True,
                    stop=True,
                )
            nc.vector.tensor_copy(out=bo_bc[:, 1024 * c : 1024 * c + 1024], in_=bank[:])

        def quantise(src, width, tag, bufs=2):
            codes = cod.tile([P, width], U32, tag=tag + "c", name=tag + "c", align_bytes=64, bufs=bufs)
            scales = cod.tile([P, width], U8, tag=tag + "s", name=tag + "s", align_bytes=64, bufs=bufs)
            nc.vector.quantize_mx(out=codes[:].bitcast(FP8X4), scales=scales[:], in_=src[:])
            return codes, scales

        def mm1(g):
            wc, ws = w3c[g]
            ac, as_ = hc[g]
            xs[g] = []
            for half in range(2):
                x = xp.tile([P, 512], F32, tag="x", name="x")
                xs[g].append(x)
                for i in range(2):
                    t = 2 * half + i
                    nc.tensor.matmul_mx(
                        out=x[:, 256 * i : 256 * i + 256],
                        lhsT=wc[:, 128 * t : 128 * t + 128].bitcast(FP8X4),
                        lhsT_scale=ws[:, 128 * t : 128 * t + 128],
                        rhs=ac[:].bitcast(FP8X4),
                        rhs_scale=as_[:],
                        start=True,
                        stop=True,
                    )

        def relu(g):
            r = res.tile([P, 4 * B], F32, tag="r", name="r")
            rs[g] = r
            for t in range(4):
                nc.scalar.activation(
                    out=r[:, 256 * t : 256 * t + 256],
                    in_=xs[g][t // 2][:, 256 * (t % 2) : 256 * (t % 2) + 256],
                    func=RELU,
                    bias=b3c[:, 4 * g + t : 4 * g + t + 1],
                    scale=1.0,
                )

        def residual(g):
            s = grp.tile([P, 4 * B], BF16, tag="h3g", name="h3g", align_bytes=64)
            h3g[g] = s
            nc.vector.tensor_tensor(
                out=s[:].rearrange("p (c i t) -> p c t i", i=4, t=4),
                in0=rs[g][:].rearrange("p (t c i) -> p c t i", t=4, i=4),
                in1=grouped[(g, "h")][:].rearrange("p (c i t) -> p c t i", i=4, t=4),
                op=ADD,
            )

        def mm2(g):
            ac, as_ = h3c[g]
            wc, ws = woc[g]
            ys[g] = []
            for bb in range(2):
                y = yp.tile([P, PD], F32, tag="y", name="y")
                ys[g].append(y)
                nc.tensor.matmul_mx(
                    out=y[:],
                    lhsT=ac[:, 128 * bb : 128 * bb + 128].bitcast(FP8X4),
                    lhsT_scale=as_[:, 128 * bb : 128 * bb + 128],
                    rhs=wc[:].bitcast(FP8X4),
                    rhs_scale=ws[:],
                    start=True,
                    stop=True,
                )

        def add_bias(g):
            if g % 2 == 0:
                ots[g // 2] = res.tile([P, 2 * 2 * PD], F32, tag="ot", name="ot", bufs=3)
            ot = ots[g // 2][:].rearrange("p (bb c) -> p bb c", bb=2)
            c0 = PD * (g % 2)
            for bb in range(2):
                nc.vector.tensor_tensor(
                    out=ot[:, bb, c0 : c0 + PD].rearrange("p (q r) -> p q r", r=4),
                    in0=ys[g][bb][:].rearrange("p (r q) -> p q r", r=4),
                    in1=bo_bc[:, PD * g : PD * g + PD].rearrange("p (q r) -> p q r", r=4),
                    op=ADD,
                )
                if g == G - 1:
                    nc.sync.dma_start(
                        out=out_view[:, bb, PD * g : PD * g + PD], in_=ot[:, bb, c0 : c0 + PD]
                    )

        def store(g0, g1):
            ot = ots[g0 // 2][:].rearrange("p (bb c) -> p bb c", bb=2)
            c0 = PD * (g0 % 2)
            nc.sync.dma_start(
                out=out_view[:, :, PD * g0 : PD * g1], in_=ot[:, :, c0 : c0 + PD * (g1 - g0)]
            )

        for g in range(LOOKAHEAD):
            load_w(g)
        spread_bias(0)
        flip(0, 0)
        flip(0, 1)
        bias3_to_partitions()
        flip(0, 2)

        for j in range(G + 3):
            if j + LOOKAHEAD < G:
                load_w(j + LOOKAHEAD)
            if 0 <= j - 2 < G:
                residual(j - 2)
            if 0 <= j - 1 < G:
                woc[j - 1] = quantise(grouped[(j - 1, "wo")], PD, "wo", bufs=3)
            if 0 <= j - 2 < G:
                h3c[j - 2] = quantise(h3g[j - 2], B, "h3")
            copy_out(j, 0)
            copy_out(j, 1)
            if j == 0:
                flip(0, 3)
            if 0 <= j - 1 < G:
                mm1(j - 1)
            copy_out(j, 2)
            copy_out(j, 3)
            flip(j, 4)
            copy_out(j, 4)
            if j < G:
                w3c[j] = quantise(grouped[(j, "w3")], H, "w3")
                hc[j] = quantise(grouped[(j, "h")], B, "h")
            flip(j + 1, 0)
            flip(j + 1, 1)
            if 0 <= j - 1 < G:
                relu(j - 1)
            g = j - 3
            if 0 <= g < G:
                mm2(g)
                add_bias(g)
                if g < G - 2 and g % 2 == 1:
                    store(g - 1, g + 1)
                if g == G - 2:
                    store(g, g + 1)
            flip(j + 1, 2)
            flip(j + 1, 3)
            for c in HEAD_BIAS.get(j, ()):
                spread_bias(c)
